import numpy as np
import ml_dtypes


def mxq(x, axis, fmt="e4m3"):
    dtype, down = {"e4m3": (ml_dtypes.float8_e4m3fn, 7), "e5m2": (ml_dtypes.float8_e5m2, 14)}[fmt]
    v = np.moveaxis(np.asarray(x, np.float32).astype(ml_dtypes.bfloat16).astype(np.float64), axis, -1)
    blocks = v.reshape(v.shape[:-1] + (-1, 32))
    amax = np.abs(blocks).max(-1, keepdims=True)
    byte = np.maximum(np.where(amax > 0, np.frexp(amax)[1] - 1 + 127, 0) - down, 1)
    scale = np.exp2(byte - 127.0)
    codes = (blocks / scale).astype(np.float32).astype(dtype).astype(np.float64)
    return np.moveaxis((codes * scale).reshape(v.shape), -1, axis)


WIDE = False


def mx_kscale(k):
    if not WIDE:
        return np.ones(k)
    levels = np.array([10, -10, 5, -5, 0])
    a = np.random.permutation(np.resize(levels, k // 512 * 4)).reshape(k // 512, 4)
    idx = np.arange(k)
    return np.exp2(a[idx // 512, idx % 128 // 32])


BF16 = ml_dtypes.bfloat16


def bf(x):
    return np.asarray(x, np.float32).astype(BF16)


def f64(x):
    return np.asarray(x).astype(np.float64)


E2M1 = np.array([0.0, 0.5, 1.0, 1.5, 2.0, 3.0, 4.0, 6.0, -0.0, -0.5, -1.0, -1.5, -2.0, -3.0, -4.0, -6.0])


def pack_weight(w, fmt):
    k, n = w.shape
    w = f64(bf(w)).reshape(k // 32, 32, n)
    amax = np.abs(w).max(1)
    if fmt == "e4m3":
        byte = np.frexp(amax)[1] - 1 + 127 - 7
    else:
        mant, ex = np.frexp(amax / 6.0)
        byte = np.where(mant > 0.5, ex, ex - 1) + 127
    byte = np.clip(np.where(amax > 0, byte, 1), 1, 254)
    scaled = (w * np.exp2(127.0 - byte)[:, None, :]).reshape(k, n).astype(np.float32)
    by_word = np.ascontiguousarray(scaled.reshape(k // 512, 128, 4, n).transpose(0, 1, 3, 2))
    if fmt == "e4m3":
        words = by_word.astype(ml_dtypes.float8_e4m3fn).view(np.uint8)
    else:
        c = by_word.astype(ml_dtypes.float4_e2m1fn).view(np.uint8) & 0xF
        words = c[..., 0::2] | (c[..., 1::2] << 4)
    return np.ascontiguousarray(words), np.ascontiguousarray(byte.astype(np.uint8).reshape(k // 512, 16, n))


def unpack_weight(words, scales, fmt):
    g, p, n, _ = words.shape
    if fmt == "e4m3":
        vals = np.ascontiguousarray(words).view(ml_dtypes.float8_e4m3fn).astype(np.float64)
    else:
        nib = np.empty((g, p, n, 4), np.uint8)
        nib[..., 0::2] = words & 0xF
        nib[..., 1::2] = words >> 4
        vals = E2M1[nib]
    vals = vals * np.repeat(np.exp2(scales.astype(np.float64) - 127.0), 8, axis=1)[..., None]
    return vals.transpose(0, 1, 3, 2).reshape(g * 512, n)

def pack4(w):
    words, scales = pack_weight(w, "e2m1")
    return words.reshape(words.shape[0], 128, -1), scales


def unpack4(words, scales):
    return unpack_weight(words.reshape(words.shape[0], 128, -1, 2), scales, "e2m1")


B, L, H = 2, 1024, 1024
HH = H // 2
BASE = 10000.0


def rope_tables():
    inv_freq = 1.0 / BASE ** (np.arange(0, H, 2) / H)
    freqs = np.outer(np.arange(L), inv_freq)
    emb = np.concatenate([freqs, freqs], axis=-1)
    return np.cos(emb), np.sin(emb)


def rotate_half(x):
    x1, x2 = np.split(x, 2, axis=-1)
    return np.concatenate([-x2, x1], axis=-1)


def setup_inputs():
    sh = mx_kscale(H)[:HH]
    s = np.concatenate([sh, sh])
    cos, sin = rope_tables()
    hidden_states = bf(np.random.standard_normal((B, L, H)) * 0.2 * s)
    w = np.random.standard_normal((H, H)) * 0.5 / np.sqrt(H) / s[None, :]
    words, scales = pack4(np.ascontiguousarray(w.T))
    return {"hidden_states": hidden_states,
            "W_q_words": words, "W_q_scales": scales,
            "cos": bf(cos), "sin": bf(sin)}


def reference(hidden_states, W_q_words, W_q_scales, cos, sin):
    x = f64(hidden_states)
    h = x * f64(cos)[None, :, :] + rotate_half(x) * f64(sin)[None, :, :]
    return mxq(h, 2, "e4m3") @ unpack4(W_q_words, W_q_scales)

@@ -1,0 +1,168 @@
+from contextlib import ExitStack
+
+import concourse.mybir as mybir
+from concourse.masks import make_identity
+
+F32 = mybir.dt.float32
+BF16 = mybir.dt.bfloat16
+I32 = mybir.dt.int32
+U32 = mybir.dt.uint32
+U8 = mybir.dt.uint8
+FP8X4 = mybir.dt.float8_e4m3fn_x4
+FP4X4 = mybir.dt.float4_e2m1fn_x4
+
+B, L, H = 2, 1024, 1024
+HALF = H // 2
+P = 128
+PACK = 4
+K_PASS = P * PACK
+PASSES = H // K_PASS
+WORDS = H // PACK
+N_TILE = 512
+N_TILES = H // N_TILE
+ROUNDS = L // P
+TILES = ROUNDS * B
+COS, SIN = 0, 1
+
+FLOPS = 2 * B * L * H * H
+
+
+def tile_denseattentiononehead_pa_kernel(
+    tc, hidden_states, W_q_words, W_q_scales, cos, sin, out
+):
+    nc = tc.nc
+
+    x_rows = hidden_states.rearrange("b (p r) j -> b p r j", r=ROUNDS)
+    cos_rows = cos.rearrange("(p r) j -> p r j", r=ROUNDS)
+    sin_rows = sin.rearrange("(p r) j -> p r j", r=ROUNDS)
+    out_rows = out.rearrange("b (p r) o -> b p r o", r=ROUNDS)
+
+    with ExitStack() as ctx:
+        resident = ctx.enter_context(tc.tile_pool(name="resident", bufs=1))
+        stream = ctx.enter_context(tc.tile_pool(name="stream", bufs=3))
+        results = ctx.enter_context(tc.tile_pool(name="results", bufs=4))
+        psum = ctx.enter_context(tc.psum_pool(name="psum", bufs=4))
+        ctx.enter_context(tc.manual_schedule())
+
+        identity = resident.tile([P, P], F32)
+        make_identity(nc, identity[:])
+
+        w_words = resident.tile([P, PASSES, 2 * H], U8, align_bytes=64)
+        w_scales = resident.tile([P, PASSES, H], U8, align_bytes=64)
+        nc.vector.memset(w_scales[:].rearrange("p g n -> p (g n)").bitcast(I32), 0)
+
+        def load_weight():
+            nc.sync.dma_start(
+                out=w_words[:].bitcast(I32),
+                in_=W_q_words.rearrange("g p n -> p g n").bitcast(I32),
+            )
+            for quadrant in range(4):
+                nc.sync.dma_start(
+                    out=w_scales[32 * quadrant : 32 * quadrant + 4, :, :].bitcast(I32),
+                    in_=W_q_scales[:, 4 * quadrant : 4 * quadrant + 4, :]
+                    .rearrange("g q n -> q g n")
+                    .bitcast(I32),
+                )
+
+        x_tiles = {}
+        tables = {}
+        for r in range(ROUNDS):
+            table = resident.tile([P, 2, H], BF16, name="table%d" % r)
+            tables[r] = table
+            x_tiles[r, 0] = resident.tile([P, H], BF16, name="x%d_0" % r)
+            x_tiles[r, 1] = resident.tile([P, H], BF16, name="x%d_1" % r)
+            nc.sync.dma_start(out=table[:, SIN, HALF:], in_=sin_rows[:, r, :HALF])
+            nc.sync.dma_start(out=table[:, SIN, :HALF], in_=sin_rows[:, r, HALF:])
+            nc.sync.dma_start(out=table[:, COS, :], in_=cos_rows[:, r, :])
+            nc.sync.dma_start(out=x_tiles[r, 0][:], in_=x_rows[0, :, r, :])
+            nc.sync.dma_start(out=x_tiles[r, 1][:], in_=x_rows[1, :, r, :])
+            if r == 0:
+                load_weight()
+
+        products = {}
+        codes = {}
+        scales = {}
+
+        def negate_sin(r):
+            nc.scalar.mul(out=tables[r][:, SIN, HALF:], in_=tables[r][:, SIN, HALF:], mul=-1.0)
+
+        def multiply_by_tables(i):
+            r, b = divmod(i, B)
+            product = stream.tile([P, 2, PACK, WORDS], F32, name="product")
+            products[i] = product
+            nc.vector.tensor_tensor(
+                out=product[:],
+                in0=x_tiles[r, b][:]
+                .rearrange("p (q t) -> p t q", t=PACK)
+                .unsqueeze(1)
+                .to_broadcast([P, 2, PACK, WORDS]),
+                in1=tables[r][:].rearrange("p a (q t) -> p a t q", t=PACK),
+                op=mybir.AluOpType.mult,
+            )
+
+        def transpose_and_add(i):
+            product = products[i]
+            grouped = stream.tile([P, PASSES, P, PACK], BF16, name="grouped", align_bytes=64)
+            for g in range(PASSES):
+                own = slice(P * g, P * (g + 1))
+                other = slice(P * (1 - g), P * (2 - g))
+                h_t = psum.tile([P, PACK, P], F32, name="h_t")
+                for t in range(PACK):
+                    nc.tensor.matmul(
+                        out=h_t[:, t, :],
+                        lhsT=product[:, COS, t, own],
+                        rhs=identity[:],
+                        is_transpose=True,
+                        start=True,
+                        stop=False,
+                    )
+                    nc.tensor.matmul(
+                        out=h_t[:, t, :],
+                        lhsT=product[:, SIN, t, other],
+                        rhs=identity[:],
+                        is_transpose=True,
+                        start=False,
+                        stop=True,
+                    )
+                nc.scalar.copy(out=grouped[:, g, :, :], in_=h_t[:].rearrange("p t l -> p l t"))
+            return grouped
+
+        def quantise(i, grouped):
+            codes[i] = stream.tile([P, PASSES * P], U32, name="codes", align_bytes=64)
+            scales[i] = stream.tile([P, PASSES * P], U8, name="scales", align_bytes=64)
+            nc.vector.quantize_mx(
+                out=codes[i][:].bitcast(FP8X4),
+                scales=scales[i][:],
+                in_=grouped[:].rearrange("p g l t -> p (g l t)"),
+            )
+
+        def project_and_store(i):
+            r, b = divmod(i, B)
+            result = results.tile([P, H], F32, name="result")
+            for n in range(N_TILES):
+                acc = psum.tile([P, N_TILE], F32, name="acc")
+                for g in range(PASSES):
+                    nc.tensor.matmul_mx(
+                        out=acc[:],
+                        lhsT=codes[i][:, P * g : P * (g + 1)].bitcast(FP8X4),
+                        lhsT_scale=scales[i][:, P * g : P * (g + 1)],
+                        rhs=w_words[:, g, 2 * N_TILE * n : 2 * N_TILE * (n + 1)].bitcast(FP4X4),
+                        rhs_scale=w_scales[:, g, N_TILE * n : N_TILE * (n + 1)],
+                        start=(g == 0),
+                        stop=(g == PASSES - 1),
+                    )
+                nc.scalar.copy(out=result[:, N_TILE * n : N_TILE * (n + 1)], in_=acc[:])
+            nc.sync.dma_start(out=out_rows[b, :, r, :], in_=result[:])
+
+        grouped_tiles = {}
+        negate_sin(0)
+        for step in range(TILES + 2):
+            if step < TILES:
+                if step % B == 0 and step // B + 1 < ROUNDS:
+                    negate_sin(step // B + 1)
+                multiply_by_tables(step)
+            if 1 <= step <= TILES:
+                grouped_tiles[step - 1] = transpose_and_add(step - 1)
+            if step >= 2:
+                quantise(step - 2, grouped_tiles[step - 2])
+                project_and_store(step - 2)

@@ -39,7 +39,7 @@ def tile_denseattentiononehead_pa_kernel(
 
     with ExitStack() as ctx:
         resident = ctx.enter_context(tc.tile_pool(name="resident", bufs=1))
-        stream = ctx.enter_context(tc.tile_pool(name="stream", bufs=3))
+        stream = ctx.enter_context(tc.tile_pool(name="stream", bufs=4))
         results = ctx.enter_context(tc.tile_pool(name="results", bufs=4))
         psum = ctx.enter_context(tc.psum_pool(name="psum", bufs=4))
         ctx.enter_context(tc.manual_schedule())
@@ -156,13 +156,16 @@ def tile_denseattentiononehead_pa_kernel(
 
         grouped_tiles = {}
         negate_sin(0)
-        for step in range(TILES + 2):
+        for step in range(TILES + 3):
+            if step >= 3:
+                quantise(step - 3, grouped_tiles[step - 3])
             if step < TILES:
                 if step % B == 0 and step // B + 1 < ROUNDS:
                     negate_sin(step // B + 1)
                 multiply_by_tables(step)
+            if step % 2 == 1 and step >= 3:
+                project_and_store(step - 3)
             if 1 <= step <= TILES:
                 grouped_tiles[step - 1] = transpose_and_add(step - 1)
-            if step >= 2:
-                quantise(step - 2, grouped_tiles[step - 2])
-                project_and_store(step - 2)
+            if step % 2 == 0 and step >= 3:
+                project_and_store(step - 3)

@@ -26,6 +26,17 @@ COS, SIN = 0, 1
 
 FLOPS = 2 * B * L * H * H
 
+LAG_Q = 3
+Q_FIRST = True
+ALTERNATE = False
+G_OUTER = False
+STREAM_BUFS = 4
+RESULT_BUFS = 6
+SPLIT_HEAD = False
+SPLIT_TAIL = True
+LAST_ADDS = True
+HALF_PACK = PACK // 2
+
 
 def tile_denseattentiononehead_pa_kernel(
     tc, hidden_states, W_q_words, W_q_scales, cos, sin, out
@@ -39,8 +50,8 @@ def tile_denseattentiononehead_pa_kernel(
 
     with ExitStack() as ctx:
         resident = ctx.enter_context(tc.tile_pool(name="resident", bufs=1))
-        stream = ctx.enter_context(tc.tile_pool(name="stream", bufs=4))
-        results = ctx.enter_context(tc.tile_pool(name="results", bufs=4))
+        stream = ctx.enter_context(tc.tile_pool(name="stream", bufs=STREAM_BUFS))
+        results = ctx.enter_context(tc.tile_pool(name="results", bufs=RESULT_BUFS))
         psum = ctx.enter_context(tc.psum_pool(name="psum", bufs=4))
         ctx.enter_context(tc.manual_schedule())
 
@@ -71,10 +82,18 @@ def tile_denseattentiononehead_pa_kernel(
             tables[r] = table
             x_tiles[r, 0] = resident.tile([P, H], BF16, name="x%d_0" % r)
             x_tiles[r, 1] = resident.tile([P, H], BF16, name="x%d_1" % r)
-            nc.sync.dma_start(out=table[:, SIN, HALF:], in_=sin_rows[:, r, :HALF])
-            nc.sync.dma_start(out=table[:, SIN, :HALF], in_=sin_rows[:, r, HALF:])
-            nc.sync.dma_start(out=table[:, COS, :], in_=cos_rows[:, r, :])
-            nc.sync.dma_start(out=x_tiles[r, 0][:], in_=x_rows[0, :, r, :])
+            if r == 0 and SPLIT_HEAD:
+                nc.sync.dma_start(out=x_tiles[0, 0][:, :HALF], in_=x_rows[0, :, 0, :HALF])
+                nc.sync.dma_start(out=table[:, COS, :HALF], in_=cos_rows[:, 0, :HALF])
+                nc.sync.dma_start(out=table[:, SIN, :HALF], in_=sin_rows[:, 0, HALF:])
+                nc.sync.dma_start(out=table[:, SIN, HALF:], in_=sin_rows[:, 0, :HALF])
+                nc.sync.dma_start(out=x_tiles[0, 0][:, HALF:], in_=x_rows[0, :, 0, HALF:])
+                nc.sync.dma_start(out=table[:, COS, HALF:], in_=cos_rows[:, 0, HALF:])
+            else:
+                nc.sync.dma_start(out=table[:, SIN, HALF:], in_=sin_rows[:, r, :HALF])
+                nc.sync.dma_start(out=table[:, SIN, :HALF], in_=sin_rows[:, r, HALF:])
+                nc.sync.dma_start(out=table[:, COS, :], in_=cos_rows[:, r, :])
+                nc.sync.dma_start(out=x_tiles[r, 0][:], in_=x_rows[0, :, r, :])
             nc.sync.dma_start(out=x_tiles[r, 1][:], in_=x_rows[1, :, r, :])
             if r == 0:
                 load_weight()
@@ -86,19 +105,61 @@ def tile_denseattentiononehead_pa_kernel(
         def negate_sin(r):
             nc.scalar.mul(out=tables[r][:, SIN, HALF:], in_=tables[r][:, SIN, HALF:], mul=-1.0)
 
+        def multiply_in_order(i):
+            r, b = divmod(i, B)
+            product = stream.tile([P, 2, H], F32, name="product")
+            products[i] = product
+            nc.vector.tensor_tensor(
+                out=product[:],
+                in0=x_tiles[r, b][:].unsqueeze(1).to_broadcast([P, 2, H]),
+                in1=tables[r][:],
+                op=mybir.AluOpType.mult,
+            )
+
+        def add_and_transpose_words(i):
+            product = products[i]
+            h_rows = stream.tile([P, H], BF16, name="h_rows", align_bytes=64)
+            words = h_rows[:].bitcast(F32)
+            grouped = stream.tile([P, PASSES, P, PACK], BF16, name="grouped", align_bytes=64)
+            h_w = psum.tile([P, PASSES, HALF_PACK, P], F32, name="h_t")
+            for g in range(PASSES):
+                nc.vector.tensor_tensor(
+                    out=h_rows[:, HALF * g : HALF * (g + 1)],
+                    in0=product[:, COS, HALF * g : HALF * (g + 1)],
+                    in1=product[:, SIN, HALF * (1 - g) : HALF * (2 - g)],
+                    op=mybir.AluOpType.add,
+                )
+                for u in range(HALF_PACK):
+                    nc.tensor.matmul(
+                        out=h_w[:, g, u, :],
+                        lhsT=words[:, HALF_PACK * P * g + u : HALF_PACK * P * (g + 1) : HALF_PACK],
+                        rhs=identity[:],
+                        is_transpose=True,
+                        start=True,
+                        stop=True,
+                    )
+            nc.scalar.copy(out=grouped[:].bitcast(F32), in_=h_w[:].rearrange("p g u l -> p g l u"))
+            return grouped
+
         def multiply_by_tables(i):
             r, b = divmod(i, B)
             product = stream.tile([P, 2, PACK, WORDS], F32, name="product")
             products[i] = product
-            nc.vector.tensor_tensor(
-                out=product[:],
-                in0=x_tiles[r, b][:]
-                .rearrange("p (q t) -> p t q", t=PACK)
-                .unsqueeze(1)
-                .to_broadcast([P, 2, PACK, WORDS]),
-                in1=tables[r][:].rearrange("p a (q t) -> p a t q", t=PACK),
-                op=mybir.AluOpType.mult,
-            )
+            pieces = [slice(0, WORDS)]
+            if i == 0 and SPLIT_HEAD:
+                pieces = [slice(0, P), slice(P, WORDS)]
+            for q in pieces:
+                j = slice(PACK * q.start, PACK * q.stop)
+                width = q.stop - q.start
+                nc.vector.tensor_tensor(
+                    out=product[:, :, :, q],
+                    in0=x_tiles[r, b][:, j]
+                    .rearrange("p (q t) -> p t q", t=PACK)
+                    .unsqueeze(1)
+                    .to_broadcast([P, 2, PACK, width]),
+                    in1=tables[r][:, :, j].rearrange("p a (q t) -> p a t q", t=PACK),
+                    op=mybir.AluOpType.mult,
+                )
 
         def transpose_and_add(i):
             product = products[i]
@@ -138,34 +199,58 @@ def tile_denseattentiononehead_pa_kernel(
 
         def project_and_store(i):
             r, b = divmod(i, B)
+            last = SPLIT_TAIL and i == TILES - 1
             result = results.tile([P, H], F32, name="result")
+            accs = {}
             for n in range(N_TILES):
-                acc = psum.tile([P, N_TILE], F32, name="acc")
-                for g in range(PASSES):
-                    nc.tensor.matmul_mx(
-                        out=acc[:],
-                        lhsT=codes[i][:, P * g : P * (g + 1)].bitcast(FP8X4),
-                        lhsT_scale=scales[i][:, P * g : P * (g + 1)],
-                        rhs=w_words[:, g, 2 * N_TILE * n : 2 * N_TILE * (n + 1)].bitcast(FP4X4),
-                        rhs_scale=w_scales[:, g, N_TILE * n : N_TILE * (n + 1)],
-                        start=(g == 0),
-                        stop=(g == PASSES - 1),
-                    )
-                nc.scalar.copy(out=result[:, N_TILE * n : N_TILE * (n + 1)], in_=acc[:])
-            nc.sync.dma_start(out=out_rows[b, :, r, :], in_=result[:])
+                accs[n] = psum.tile([P, N_TILE], F32, name="acc")
+            if G_OUTER:
+                order = [(g, n) for g in range(PASSES) for n in range(N_TILES)]
+            else:
+                order = [(g, n) for n in range(N_TILES) for g in range(PASSES)]
+            for g, n in order:
+                nc.tensor.matmul_mx(
+                    out=accs[n][:],
+                    lhsT=codes[i][:, P * g : P * (g + 1)].bitcast(FP8X4),
+                    lhsT_scale=scales[i][:, P * g : P * (g + 1)],
+                    rhs=w_words[:, g, 2 * N_TILE * n : 2 * N_TILE * (n + 1)].bitcast(FP4X4),
+                    rhs_scale=w_scales[:, g, N_TILE * n : N_TILE * (n + 1)],
+                    start=(g == 0),
+                    stop=(g == PASSES - 1),
+                )
+                if g == PASSES - 1:
+                    pieces = 2 if last and n == N_TILES - 1 else 1
+                    width = N_TILE // pieces
+                    for piece in range(pieces):
+                        columns = slice(N_TILE * n + width * piece, N_TILE * n + width * (piece + 1))
+                        nc.scalar.copy(
+                            out=result[:, columns], in_=accs[n][:, width * piece : width * (piece + 1)]
+                        )
+                        if last:
+                            nc.sync.dma_start(out=out_rows[b, :, r, columns], in_=result[:, columns])
+            if not last:
+                nc.sync.dma_start(out=out_rows[b, :, r, :], in_=result[:])
 
         grouped_tiles = {}
         negate_sin(0)
-        for step in range(TILES + 3):
-            if step >= 3:
-                quantise(step - 3, grouped_tiles[step - 3])
+        for step in range(TILES + LAG_Q):
+            if Q_FIRST and step >= LAG_Q:
+                quantise(step - LAG_Q, grouped_tiles[step - LAG_Q])
             if step < TILES:
                 if step % B == 0 and step // B + 1 < ROUNDS:
                     negate_sin(step // B + 1)
-                multiply_by_tables(step)
-            if step % 2 == 1 and step >= 3:
-                project_and_store(step - 3)
-            if 1 <= step <= TILES:
+                if LAST_ADDS and step == TILES - 1:
+                    multiply_in_order(step)
+                else:
+                    multiply_by_tables(step)
+            if not Q_FIRST and step >= LAG_Q:
+                quantise(step - LAG_Q, grouped_tiles[step - LAG_Q])
+            mx_first = (ALTERNATE and step % 2 == 1) or (LAST_ADDS and step == TILES)
+            if mx_first and step >= LAG_Q:
+                project_and_store(step - LAG_Q)
+            if LAST_ADDS and step == TILES:
+                grouped_tiles[step - 1] = add_and_transpose_words(step - 1)
+            elif 1 <= step <= TILES:
                 grouped_tiles[step - 1] = transpose_and_add(step - 1)
-            if step % 2 == 0 and step >= 3:
-                project_and_store(step - 3)
+            if not mx_first and step >= LAG_Q:
+                project_and_store(step - LAG_Q)

@@ -99,6 +99,7 @@ def tile_denseattentiononehead_pa_kernel(
                 load_weight()
 
         products = {}
+        sums = {}
         codes = {}
         scales = {}
 
@@ -116,12 +117,10 @@ def tile_denseattentiononehead_pa_kernel(
                 op=mybir.AluOpType.mult,
             )
 
-        def add_and_transpose_words(i):
+        def add_products(i):
             product = products[i]
             h_rows = stream.tile([P, H], BF16, name="h_rows", align_bytes=64)
-            words = h_rows[:].bitcast(F32)
-            grouped = stream.tile([P, PASSES, P, PACK], BF16, name="grouped", align_bytes=64)
-            h_w = psum.tile([P, PASSES, HALF_PACK, P], F32, name="h_t")
+            sums[i] = h_rows
             for g in range(PASSES):
                 nc.vector.tensor_tensor(
                     out=h_rows[:, HALF * g : HALF * (g + 1)],
@@ -129,6 +128,12 @@ def tile_denseattentiononehead_pa_kernel(
                     in1=product[:, SIN, HALF * (1 - g) : HALF * (2 - g)],
                     op=mybir.AluOpType.add,
                 )
+
+        def transpose_words(i):
+            words = sums[i][:].bitcast(F32)
+            grouped = stream.tile([P, PASSES, P, PACK], BF16, name="grouped", align_bytes=64)
+            h_w = psum.tile([P, PASSES, HALF_PACK, P], F32, name="h_t")
+            for g in range(PASSES):
                 for u in range(HALF_PACK):
                     nc.tensor.matmul(
                         out=h_w[:, g, u, :],
@@ -241,15 +246,16 @@ def tile_denseattentiononehead_pa_kernel(
                     negate_sin(step // B + 1)
                 if LAST_ADDS and step == TILES - 1:
                     multiply_in_order(step)
+                    add_products(step)
                 else:
                     multiply_by_tables(step)
             if not Q_FIRST and step >= LAG_Q:
                 quantise(step - LAG_Q, grouped_tiles[step - LAG_Q])
-            mx_first = (ALTERNATE and step % 2 == 1) or (LAST_ADDS and step == TILES)
+            mx_first = ALTERNATE and step % 2 == 1
             if mx_first and step >= LAG_Q:
                 project_and_store(step - LAG_Q)
             if LAST_ADDS and step == TILES:
-                grouped_tiles[step - 1] = add_and_transpose_words(step - 1)
+                grouped_tiles[step - 1] = transpose_words(step - 1)
             elif 1 <= step <= TILES:
                 grouped_tiles[step - 1] = transpose_and_add(step - 1)
             if not mx_first and step >= LAG_Q:

@@ -35,6 +35,7 @@ RESULT_BUFS = 6
 SPLIT_HEAD = False
 SPLIT_TAIL = True
 LAST_ADDS = True
+WARM_UP = 4
 HALF_PACK = PACK // 2
 
 
@@ -235,6 +236,12 @@ def tile_denseattentiononehead_pa_kernel(
                             nc.sync.dma_start(out=out_rows[b, :, r, columns], in_=result[:, columns])
             if not last:
                 nc.sync.dma_start(out=out_rows[b, :, r, :], in_=result[:])
+
+        warm = psum.tile([P, N_TILE], F32, name="acc")
+        for k in range(WARM_UP):
+            nc.tensor.matmul(
+                out=warm[:], lhsT=x_tiles[0, 0][:, :P], rhs=x_tiles[0, 0][:, :N_TILE], start=True, stop=True
+            )
 
         grouped_tiles = {}
         negate_sin(0)

@@ -10,33 +10,24 @@ U32 = mybir.dt.uint32
 U8 = mybir.dt.uint8
 FP8X4 = mybir.dt.float8_e4m3fn_x4
 FP4X4 = mybir.dt.float4_e2m1fn_x4
+MULT = mybir.AluOpType.mult
+ADD = mybir.AluOpType.add
+SUBTRACT = mybir.AluOpType.subtract
 
 B, L, H = 2, 1024, 1024
 HALF = H // 2
 P = 128
 PACK = 4
-K_PASS = P * PACK
-PASSES = H // K_PASS
-WORDS = H // PACK
+PAIRS = PACK // 2
+PASSES = H // (P * PACK)
 N_TILE = 512
 N_TILES = H // N_TILE
 ROUNDS = L // P
 TILES = ROUNDS * B
 COS, SIN = 0, 1
+WARM_UP = 4
 
 FLOPS = 2 * B * L * H * H
-
-LAG_Q = 3
-Q_FIRST = True
-ALTERNATE = False
-G_OUTER = False
-STREAM_BUFS = 4
-RESULT_BUFS = 6
-SPLIT_HEAD = False
-SPLIT_TAIL = True
-LAST_ADDS = True
-WARM_UP = 4
-HALF_PACK = PACK // 2
 
 
 def tile_denseattentiononehead_pa_kernel(
@@ -51,9 +42,11 @@ def tile_denseattentiononehead_pa_kernel(
 
     with ExitStack() as ctx:
         resident = ctx.enter_context(tc.tile_pool(name="resident", bufs=1))
-        stream = ctx.enter_context(tc.tile_pool(name="stream", bufs=STREAM_BUFS))
-        results = ctx.enter_context(tc.tile_pool(name="results", bufs=RESULT_BUFS))
-        psum = ctx.enter_context(tc.psum_pool(name="psum", bufs=4))
+        stream = ctx.enter_context(tc.tile_pool(name="stream", bufs=4))
+        results = ctx.enter_context(tc.tile_pool(name="results", bufs=6))
+        psum_x = ctx.enter_context(tc.psum_pool(name="psum_x", bufs=2))
+        psum_tables = ctx.enter_context(tc.psum_pool(name="psum_tables", bufs=2))
+        psum_acc = ctx.enter_context(tc.psum_pool(name="psum_acc", bufs=4))
         ctx.enter_context(tc.manual_schedule())
 
         identity = resident.tile([P, P], F32)
@@ -83,187 +76,146 @@ def tile_denseattentiononehead_pa_kernel(
             tables[r] = table
             x_tiles[r, 0] = resident.tile([P, H], BF16, name="x%d_0" % r)
             x_tiles[r, 1] = resident.tile([P, H], BF16, name="x%d_1" % r)
-            if r == 0 and SPLIT_HEAD:
-                nc.sync.dma_start(out=x_tiles[0, 0][:, :HALF], in_=x_rows[0, :, 0, :HALF])
-                nc.sync.dma_start(out=table[:, COS, :HALF], in_=cos_rows[:, 0, :HALF])
-                nc.sync.dma_start(out=table[:, SIN, :HALF], in_=sin_rows[:, 0, HALF:])
-                nc.sync.dma_start(out=table[:, SIN, HALF:], in_=sin_rows[:, 0, :HALF])
-                nc.sync.dma_start(out=x_tiles[0, 0][:, HALF:], in_=x_rows[0, :, 0, HALF:])
-                nc.sync.dma_start(out=table[:, COS, HALF:], in_=cos_rows[:, 0, HALF:])
-            else:
-                nc.sync.dma_start(out=table[:, SIN, HALF:], in_=sin_rows[:, r, :HALF])
-                nc.sync.dma_start(out=table[:, SIN, :HALF], in_=sin_rows[:, r, HALF:])
-                nc.sync.dma_start(out=table[:, COS, :], in_=cos_rows[:, r, :])
-                nc.sync.dma_start(out=x_tiles[r, 0][:], in_=x_rows[0, :, r, :])
+            nc.sync.dma_start(out=table[:, COS, :], in_=cos_rows[:, r, :])
+            nc.sync.dma_start(out=table[:, SIN, :], in_=sin_rows[:, r, :])
+            nc.sync.dma_start(out=x_tiles[r, 0][:], in_=x_rows[0, :, r, :])
             nc.sync.dma_start(out=x_tiles[r, 1][:], in_=x_rows[1, :, r, :])
             if r == 0:
                 load_weight()
 
+        table_banks = {}
+        turned_tables = {}
+        x_banks = {}
         products = {}
-        sums = {}
+        grouped_tiles = {}
         codes = {}
         scales = {}
 
-        def negate_sin(r):
-            nc.scalar.mul(out=tables[r][:, SIN, HALF:], in_=tables[r][:, SIN, HALF:], mul=-1.0)
+        def transpose_words(bank, rows, swap):
+            words = rows.bitcast(F32)
+            for g in range(PASSES):
+                for u in range(PAIRS):
+                    nc.tensor.matmul(
+                        out=bank[:, 1 - g if swap else g, u, :],
+                        lhsT=words[:, PAIRS * P * g + u : PAIRS * P * (g + 1) : PAIRS],
+                        rhs=identity[:],
+                        is_transpose=True,
+                        start=True,
+                        stop=True,
+                    )
 
-        def multiply_in_order(i):
-            r, b = divmod(i, B)
+        def transpose_tables(r):
+            for kind in (COS, SIN):
+                bank = psum_tables.tile([P, PASSES, PAIRS, P], F32, name="table_t")
+                table_banks[r, kind] = bank
+                transpose_words(bank, tables[r][:, kind, :], kind == SIN)
+
+        def copy_tables(r):
+            turned = stream.tile([P, 2, H], BF16, name="turned")
+            turned_tables[r] = turned
+            for kind in (COS, SIN):
+                source = table_banks[r, kind][:].rearrange("p g u l -> p (g u l)")
+                target = turned[:, kind, :].bitcast(F32)
+                if r == 0 and kind == COS:
+                    nc.vector.tensor_copy(out=target, in_=source)
+                else:
+                    nc.scalar.copy(out=target, in_=source)
+
+        def transpose_x(i):
+            x_banks[i] = psum_x.tile([P, PASSES, PAIRS, P], F32, name="x_t")
+            transpose_words(x_banks[i], x_tiles[divmod(i, B)][:], False)
+
+        def multiply_by_tables(i):
             product = stream.tile([P, 2, H], F32, name="product")
             products[i] = product
             nc.vector.tensor_tensor(
                 out=product[:],
-                in0=x_tiles[r, b][:].unsqueeze(1).to_broadcast([P, 2, H]),
-                in1=tables[r][:],
-                op=mybir.AluOpType.mult,
+                in0=x_banks[i][:]
+                .rearrange("p g u l -> p (g u l)")
+                .bitcast(BF16)
+                .unsqueeze(1)
+                .to_broadcast([P, 2, H]),
+                in1=turned_tables[i // B][:],
+                op=MULT,
             )
 
-        def add_products(i):
-            product = products[i]
-            h_rows = stream.tile([P, H], BF16, name="h_rows", align_bytes=64)
-            sums[i] = h_rows
-            for g in range(PASSES):
-                nc.vector.tensor_tensor(
-                    out=h_rows[:, HALF * g : HALF * (g + 1)],
-                    in0=product[:, COS, HALF * g : HALF * (g + 1)],
-                    in1=product[:, SIN, HALF * (1 - g) : HALF * (2 - g)],
-                    op=mybir.AluOpType.add,
-                )
-
-        def transpose_words(i):
-            words = sums[i][:].bitcast(F32)
-            grouped = stream.tile([P, PASSES, P, PACK], BF16, name="grouped", align_bytes=64)
-            h_w = psum.tile([P, PASSES, HALF_PACK, P], F32, name="h_t")
-            for g in range(PASSES):
-                for u in range(HALF_PACK):
-                    nc.tensor.matmul(
-                        out=h_w[:, g, u, :],
-                        lhsT=words[:, HALF_PACK * P * g + u : HALF_PACK * P * (g + 1) : HALF_PACK],
-                        rhs=identity[:],
-                        is_transpose=True,
-                        start=True,
-                        stop=True,
-                    )
-            nc.scalar.copy(out=grouped[:].bitcast(F32), in_=h_w[:].rearrange("p g u l -> p g l u"))
-            return grouped
-
-        def multiply_by_tables(i):
-            r, b = divmod(i, B)
-            product = stream.tile([P, 2, PACK, WORDS], F32, name="product")
-            products[i] = product
-            pieces = [slice(0, WORDS)]
-            if i == 0 and SPLIT_HEAD:
-                pieces = [slice(0, P), slice(P, WORDS)]
-            for q in pieces:
-                j = slice(PACK * q.start, PACK * q.stop)
-                width = q.stop - q.start
-                nc.vector.tensor_tensor(
-                    out=product[:, :, :, q],
-                    in0=x_tiles[r, b][:, j]
-                    .rearrange("p (q t) -> p t q", t=PACK)
-                    .unsqueeze(1)
-                    .to_broadcast([P, 2, PACK, width]),
-                    in1=tables[r][:, :, j].rearrange("p a (q t) -> p a t q", t=PACK),
-                    op=mybir.AluOpType.mult,
-                )
-
-        def transpose_and_add(i):
+        def add_products(i, engine):
             product = products[i]
             grouped = stream.tile([P, PASSES, P, PACK], BF16, name="grouped", align_bytes=64)
+            grouped_tiles[i] = grouped
             for g in range(PASSES):
-                own = slice(P * g, P * (g + 1))
-                other = slice(P * (1 - g), P * (2 - g))
-                h_t = psum.tile([P, PACK, P], F32, name="h_t")
-                for t in range(PACK):
-                    nc.tensor.matmul(
-                        out=h_t[:, t, :],
-                        lhsT=product[:, COS, t, own],
-                        rhs=identity[:],
-                        is_transpose=True,
-                        start=True,
-                        stop=False,
-                    )
-                    nc.tensor.matmul(
-                        out=h_t[:, t, :],
-                        lhsT=product[:, SIN, t, other],
-                        rhs=identity[:],
-                        is_transpose=True,
-                        start=False,
-                        stop=True,
-                    )
-                nc.scalar.copy(out=grouped[:, g, :, :], in_=h_t[:].rearrange("p t l -> p l t"))
-            return grouped
+                engine.tensor_tensor(
+                    out=grouped[:, g, :, :].rearrange("p l (u e) -> p l u e", e=2),
+                    in0=product[:, COS, HALF * g : HALF * (g + 1)].rearrange("p (u l e) -> p l u e", u=PAIRS, e=2),
+                    in1=product[:, SIN, HALF * (1 - g) : HALF * (2 - g)].rearrange(
+                        "p (u l e) -> p l u e", u=PAIRS, e=2
+                    ),
+                    op=SUBTRACT if g == 0 else ADD,
+                )
 
-        def quantise(i, grouped):
+        def quantise(i):
             codes[i] = stream.tile([P, PASSES * P], U32, name="codes", align_bytes=64)
             scales[i] = stream.tile([P, PASSES * P], U8, name="scales", align_bytes=64)
             nc.vector.quantize_mx(
                 out=codes[i][:].bitcast(FP8X4),
                 scales=scales[i][:],
-                in_=grouped[:].rearrange("p g l t -> p (g l t)"),
+                in_=grouped_tiles[i][:].rearrange("p g l t -> p (g l t)"),
             )
 
         def project_and_store(i):
             r, b = divmod(i, B)
-            last = SPLIT_TAIL and i == TILES - 1
+            last = i == TILES - 1
             result = results.tile([P, H], F32, name="result")
-            accs = {}
             for n in range(N_TILES):
-                accs[n] = psum.tile([P, N_TILE], F32, name="acc")
-            if G_OUTER:
-                order = [(g, n) for g in range(PASSES) for n in range(N_TILES)]
-            else:
-                order = [(g, n) for n in range(N_TILES) for g in range(PASSES)]
-            for g, n in order:
-                nc.tensor.matmul_mx(
-                    out=accs[n][:],
-                    lhsT=codes[i][:, P * g : P * (g + 1)].bitcast(FP8X4),
-                    lhsT_scale=scales[i][:, P * g : P * (g + 1)],
-                    rhs=w_words[:, g, 2 * N_TILE * n : 2 * N_TILE * (n + 1)].bitcast(FP4X4),
-                    rhs_scale=w_scales[:, g, N_TILE * n : N_TILE * (n + 1)],
-                    start=(g == 0),
-                    stop=(g == PASSES - 1),
-                )
-                if g == PASSES - 1:
-                    pieces = 2 if last and n == N_TILES - 1 else 1
-                    width = N_TILE // pieces
-                    for piece in range(pieces):
-                        columns = slice(N_TILE * n + width * piece, N_TILE * n + width * (piece + 1))
-                        nc.scalar.copy(
-                            out=result[:, columns], in_=accs[n][:, width * piece : width * (piece + 1)]
-                        )
-                        if last:
-                            nc.sync.dma_start(out=out_rows[b, :, r, columns], in_=result[:, columns])
+                acc = psum_acc.tile([P, N_TILE], F32, name="acc")
+                for g in range(PASSES):
+                    nc.tensor.matmul_mx(
+                        out=acc[:],
+                        lhsT=codes[i][:, P * g : P * (g + 1)].bitcast(FP8X4),
+                        lhsT_scale=scales[i][:, P * g : P * (g + 1)],
+                        rhs=w_words[:, g, 2 * N_TILE * n : 2 * N_TILE * (n + 1)].bitcast(FP4X4),
+                        rhs_scale=w_scales[:, g, N_TILE * n : N_TILE * (n + 1)],
+                        start=(g == 0),
+                        stop=(g == PASSES - 1),
+                    )
+                pieces = 2 if last and n == N_TILES - 1 else 1
+                width = N_TILE // pieces
+                for piece in range(pieces):
+                    columns = slice(N_TILE * n + width * piece, N_TILE * n + width * (piece + 1))
+                    nc.scalar.copy(out=result[:, columns], in_=acc[:, width * piece : width * (piece + 1)])
+                    if last:
+                        nc.sync.dma_start(out=out_rows[b, :, r, columns], in_=result[:, columns])
             if not last:
                 nc.sync.dma_start(out=out_rows[b, :, r, :], in_=result[:])
 
-        warm = psum.tile([P, N_TILE], F32, name="acc")
+        warm = psum_acc.tile([P, N_TILE], F32, name="acc")
         for k in range(WARM_UP):
             nc.tensor.matmul(
-                out=warm[:], lhsT=x_tiles[0, 0][:, :P], rhs=x_tiles[0, 0][:, :N_TILE], start=True, stop=True
+                out=warm[:],
+                lhsT=tables[0][:, COS, :P],
+                rhs=tables[0][:, COS, :N_TILE],
+                start=True,
+                stop=True,
             )
 
-        grouped_tiles = {}
-        negate_sin(0)
-        for step in range(TILES + LAG_Q):
-            if Q_FIRST and step >= LAG_Q:
-                quantise(step - LAG_Q, grouped_tiles[step - LAG_Q])
+        transpose_tables(0)
+        copy_tables(0)
+        transpose_x(0)
+        for step in range(TILES + 3):
             if step < TILES:
-                if step % B == 0 and step // B + 1 < ROUNDS:
-                    negate_sin(step // B + 1)
-                if LAST_ADDS and step == TILES - 1:
-                    multiply_in_order(step)
-                    add_products(step)
-                else:
-                    multiply_by_tables(step)
-            if not Q_FIRST and step >= LAG_Q:
-                quantise(step - LAG_Q, grouped_tiles[step - LAG_Q])
-            mx_first = ALTERNATE and step % 2 == 1
-            if mx_first and step >= LAG_Q:
-                project_and_store(step - LAG_Q)
-            if LAST_ADDS and step == TILES:
-                grouped_tiles[step - 1] = transpose_words(step - 1)
-            elif 1 <= step <= TILES:
-                grouped_tiles[step - 1] = transpose_and_add(step - 1)
-            if not mx_first and step >= LAG_Q:
-                project_and_store(step - LAG_Q)
+                multiply_by_tables(step)
+            if 2 <= step < TILES:
+                quantise(step - 2)
+            if step < TILES - 1:
+                add_products(step, nc.gpsimd)
+            if step == TILES - 1:
+                quantise(TILES - 2)
+                add_products(TILES - 1, nc.vector)
+                quantise(TILES - 1)
+            if step + 1 < TILES:
+                transpose_x(step + 1)
+            if step % B == 0 and step // B + 1 < ROUNDS:
+                transpose_tables(step // B + 1)
+                copy_tables(step // B + 1)
+            if step >= 3:
+                project_and_store(step - 3)

@@ -12,7 +12,6 @@ FP8X4 = mybir.dt.float8_e4m3fn_x4
 FP4X4 = mybir.dt.float4_e2m1fn_x4
 MULT = mybir.AluOpType.mult
 ADD = mybir.AluOpType.add
-SUBTRACT = mybir.AluOpType.subtract
 
 B, L, H = 2, 1024, 1024
 HALF = H // 2
@@ -91,12 +90,12 @@ def tile_denseattentiononehead_pa_kernel(
         codes = {}
         scales = {}
 
-        def transpose_words(bank, rows, swap):
+        def transpose_words(bank, rows, side_by_side):
             words = rows.bitcast(F32)
             for g in range(PASSES):
                 for u in range(PAIRS):
                     nc.tensor.matmul(
-                        out=bank[:, 1 - g if swap else g, u, :],
+                        out=bank[:, g, :, u] if side_by_side else bank[:, g, u, :],
                         lhsT=words[:, PAIRS * P * g + u : PAIRS * P * (g + 1) : PAIRS],
                         rhs=identity[:],
                         is_transpose=True,
@@ -108,22 +107,35 @@ def tile_denseattentiononehead_pa_kernel(
             for kind in (COS, SIN):
                 bank = psum_tables.tile([P, PASSES, PAIRS, P], F32, name="table_t")
                 table_banks[r, kind] = bank
-                transpose_words(bank, tables[r][:, kind, :], kind == SIN)
+                transpose_words(bank, tables[r][:, kind, :], False)
 
         def copy_tables(r):
-            turned = stream.tile([P, 2, H], BF16, name="turned")
+            turned = stream.tile([P, 2, PASSES, P, PACK], BF16, name="turned")
             turned_tables[r] = turned
-            for kind in (COS, SIN):
-                source = table_banks[r, kind][:].rearrange("p g u l -> p (g u l)")
-                target = turned[:, kind, :].bitcast(F32)
-                if r == 0 and kind == COS:
-                    nc.vector.tensor_copy(out=target, in_=source)
-                else:
-                    nc.scalar.copy(out=target, in_=source)
+            bank = table_banks[r, COS]
+            target = turned[:, COS, :, :, :].rearrange("p g l t -> p (g l t)").bitcast(F32)
+            copy = nc.vector.tensor_copy if r == 0 else nc.scalar.copy
+            copy(
+                out=target.rearrange("p (g l u) -> p g l u", g=PASSES, u=PAIRS),
+                in_=bank[:].rearrange("p g u l -> p g l u"),
+            )
+            bank = table_banks[r, SIN]
+            nc.scalar.copy(
+                out=turned[:, SIN, 0, :, :].rearrange("p l t -> p (l t)").bitcast(F32).rearrange("p (l u) -> p l u", u=PAIRS),
+                in_=bank[:, 1, :, :].rearrange("p u l -> p l u"),
+            )
+            nc.scalar.mul(
+                out=turned[:, SIN, 1, :, :].rearrange("p l (u e) -> p l u e", e=2),
+                in_=bank[:, 0, :, :]
+                .rearrange("p u l -> p (u l)")
+                .bitcast(BF16)
+                .rearrange("p (u l e) -> p l u e", u=PAIRS, e=2),
+                mul=-1.0,
+            )
 
         def transpose_x(i):
-            x_banks[i] = psum_x.tile([P, PASSES, PAIRS, P], F32, name="x_t")
-            transpose_words(x_banks[i], x_tiles[divmod(i, B)][:], False)
+            x_banks[i] = psum_x.tile([P, PASSES, P, PAIRS], F32, name="x_t")
+            transpose_words(x_banks[i], x_tiles[divmod(i, B)][:], True)
 
         def multiply_by_tables(i):
             product = stream.tile([P, 2, H], F32, name="product")
@@ -131,11 +143,11 @@ def tile_denseattentiononehead_pa_kernel(
             nc.vector.tensor_tensor(
                 out=product[:],
                 in0=x_banks[i][:]
-                .rearrange("p g u l -> p (g u l)")
+                .rearrange("p g l u -> p (g l u)")
                 .bitcast(BF16)
                 .unsqueeze(1)
                 .to_broadcast([P, 2, H]),
-                in1=turned_tables[i // B][:],
+                in1=turned_tables[i // B][:].rearrange("p a g l t -> p a (g l t)"),
                 op=MULT,
             )
 
@@ -143,15 +155,12 @@ def tile_denseattentiononehead_pa_kernel(
             product = products[i]
             grouped = stream.tile([P, PASSES, P, PACK], BF16, name="grouped", align_bytes=64)
             grouped_tiles[i] = grouped
-            for g in range(PASSES):
-                engine.tensor_tensor(
-                    out=grouped[:, g, :, :].rearrange("p l (u e) -> p l u e", e=2),
-                    in0=product[:, COS, HALF * g : HALF * (g + 1)].rearrange("p (u l e) -> p l u e", u=PAIRS, e=2),
-                    in1=product[:, SIN, HALF * (1 - g) : HALF * (2 - g)].rearrange(
-                        "p (u l e) -> p l u e", u=PAIRS, e=2
-                    ),
-                    op=SUBTRACT if g == 0 else ADD,
-                )
+            engine.tensor_tensor(
+                out=grouped[:].rearrange("p g l t -> p g (l t)"),
+                in0=product[:, COS, :].rearrange("p (g w) -> p g w", g=PASSES),
+                in1=product[:, SIN, :].rearrange("p (g w) -> p g w", g=PASSES)[:, ::-1, :],
+                op=ADD,
+            )
 
         def quantise(i):
             codes[i] = stream.tile([P, PASSES * P], U32, name="codes", align_bytes=64)

@@ -24,6 +24,7 @@ N_TILES = H // N_TILE
 ROUNDS = L // P
 TILES = ROUNDS * B
 COS, SIN = 0, 1
+WORDS = H // PACK
 WARM_UP = 4
 
 FLOPS = 2 * B * L * H * H
@@ -75,11 +76,16 @@ def tile_denseattentiononehead_pa_kernel(
             tables[r] = table
             x_tiles[r, 0] = resident.tile([P, H], BF16, name="x%d_0" % r)
             x_tiles[r, 1] = resident.tile([P, H], BF16, name="x%d_1" % r)
-            nc.sync.dma_start(out=table[:, COS, :], in_=cos_rows[:, r, :])
-            nc.sync.dma_start(out=table[:, SIN, :], in_=sin_rows[:, r, :])
+            if r == 0:
+                nc.sync.dma_start(out=table[:, SIN, HALF:], in_=sin_rows[:, r, :HALF])
+                nc.sync.dma_start(out=table[:, SIN, :HALF], in_=sin_rows[:, r, HALF:])
+                nc.sync.dma_start(out=table[:, COS, :], in_=cos_rows[:, r, :])
+            else:
+                nc.sync.dma_start(out=table[:, COS, :], in_=cos_rows[:, r, :])
+                nc.sync.dma_start(out=table[:, SIN, :], in_=sin_rows[:, r, :])
             nc.sync.dma_start(out=x_tiles[r, 0][:], in_=x_rows[0, :, r, :])
             nc.sync.dma_start(out=x_tiles[r, 1][:], in_=x_rows[1, :, r, :])
-            if r == 0:
+            if r == 1:
                 load_weight()
 
         table_banks = {}
@@ -114,8 +120,7 @@ def tile_denseattentiononehead_pa_kernel(
             turned_tables[r] = turned
             bank = table_banks[r, COS]
             target = turned[:, COS, :, :, :].rearrange("p g l t -> p (g l t)").bitcast(F32)
-            copy = nc.vector.tensor_copy if r == 0 else nc.scalar.copy
-            copy(
+            nc.scalar.copy(
                 out=target.rearrange("p (g l u) -> p g l u", g=PASSES, u=PAIRS),
                 in_=bank[:].rearrange("p g u l -> p g l u"),
             )
@@ -151,16 +156,97 @@ def tile_denseattentiononehead_pa_kernel(
                 op=MULT,
             )
 
-        def add_products(i, engine):
+        def add_products(i):
             product = products[i]
             grouped = stream.tile([P, PASSES, P, PACK], BF16, name="grouped", align_bytes=64)
             grouped_tiles[i] = grouped
-            engine.tensor_tensor(
+            nc.gpsimd.tensor_tensor(
                 out=grouped[:].rearrange("p g l t -> p g (l t)"),
                 in0=product[:, COS, :].rearrange("p (g w) -> p g w", g=PASSES),
                 in1=product[:, SIN, :].rearrange("p (g w) -> p g w", g=PASSES)[:, ::-1, :],
                 op=ADD,
             )
+
+
+        def add_and_quantise_last():
+            i = TILES - 1
+            product = products[i]
+            grouped = stream.tile([P, PASSES, P, PACK], BF16, name="grouped", align_bytes=64)
+            codes[i] = stream.tile([P, PASSES * P], U32, name="codes", align_bytes=64)
+            scales[i] = stream.tile([P, PASSES * P], U8, name="scales", align_bytes=64)
+            for g in range(PASSES):
+                nc.vector.tensor_tensor(
+                    out=grouped[:, g, :, :].rearrange("p l t -> p (l t)"),
+                    in0=product[:, COS, HALF * g : HALF * (g + 1)],
+                    in1=product[:, SIN, HALF * (1 - g) : HALF * (2 - g)],
+                    op=ADD,
+                )
+            for g in range(PASSES):
+                nc.vector.quantize_mx(
+                    out=codes[i][:, P * g : P * (g + 1)].bitcast(FP8X4),
+                    scales=scales[i][:, P * g : P * (g + 1)],
+                    in_=grouped[:, g, :, :].rearrange("p l t -> p (l t)"),
+                )
+
+        def project_and_store_last():
+            i = TILES - 1
+            r, b = divmod(i, B)
+            result = results.tile([P, H], F32, name="result")
+            accs = {}
+            for n in range(N_TILES):
+                accs[n] = psum_acc.tile([P, N_TILE], F32, name="acc")
+            for g in range(PASSES):
+                for n in range(N_TILES):
+                    nc.tensor.matmul_mx(
+                        out=accs[n][:],
+                        lhsT=codes[i][:, P * g : P * (g + 1)].bitcast(FP8X4),
+                        lhsT_scale=scales[i][:, P * g : P * (g + 1)],
+                        rhs=w_words[:, g, 2 * N_TILE * n : 2 * N_TILE * (n + 1)].bitcast(FP4X4),
+                        rhs_scale=w_scales[:, g, N_TILE * n : N_TILE * (n + 1)],
+                        start=(g == 0),
+                        stop=(g == PASSES - 1),
+                    )
+            for n, copy in ((0, nc.scalar.copy), (1, nc.vector.tensor_copy)):
+                for piece in range(2):
+                    width = N_TILE // 2
+                    columns = slice(N_TILE * n + width * piece, N_TILE * n + width * (piece + 1))
+                    copy(out=result[:, columns], in_=accs[n][:, width * piece : width * (piece + 1)])
+                    nc.sync.dma_start(out=out_rows[b, :, r, columns], in_=result[:, columns])
+
+
+        def multiply_in_rows(i):
+            product = stream.tile([P, 2, PACK, WORDS], F32, name="product")
+            products[i] = product
+            nc.vector.tensor_tensor(
+                out=product[:],
+                in0=x_tiles[divmod(i, B)][:]
+                .rearrange("p (q t) -> p t q", t=PACK)
+                .unsqueeze(1)
+                .to_broadcast([P, 2, PACK, WORDS]),
+                in1=tables[i // B][:].rearrange("p a (q t) -> p a t q", t=PACK),
+                op=MULT,
+            )
+
+        def transpose_and_add(i):
+            product = products[i]
+            grouped = stream.tile([P, PASSES, P, PACK], BF16, name="grouped", align_bytes=64)
+            grouped_tiles[i] = grouped
+            for g in range(PASSES):
+                own = slice(P * g, P * (g + 1))
+                other = slice(P * (1 - g), P * (2 - g))
+                h_t = psum_acc.tile([P, PACK, P], F32, name="acc")
+                for t in range(PACK):
+                    for kind, words in ((COS, own), (SIN, other)):
+                        nc.tensor.matmul(
+                            out=h_t[:, t, :],
+                            lhsT=product[:, kind, t, words],
+                            rhs=identity[:],
+                            is_transpose=True,
+                            start=(kind == COS),
+                            stop=(kind == SIN),
+                        )
+                nc.scalar.copy(out=grouped[:, g, :, :], in_=h_t[:].rearrange("p t l -> p l t"))
+
 
         def quantise(i):
             codes[i] = stream.tile([P, PASSES * P], U32, name="codes", align_bytes=64)
@@ -173,7 +259,6 @@ def tile_denseattentiononehead_pa_kernel(
 
         def project_and_store(i):
             r, b = divmod(i, B)
-            last = i == TILES - 1
             result = results.tile([P, H], F32, name="result")
             for n in range(N_TILES):
                 acc = psum_acc.tile([P, N_TILE], F32, name="acc")
@@ -187,15 +272,8 @@ def tile_denseattentiononehead_pa_kernel(
                         start=(g == 0),
                         stop=(g == PASSES - 1),
                     )
-                pieces = 2 if last and n == N_TILES - 1 else 1
-                width = N_TILE // pieces
-                for piece in range(pieces):
-                    columns = slice(N_TILE * n + width * piece, N_TILE * n + width * (piece + 1))
-                    nc.scalar.copy(out=result[:, columns], in_=acc[:, width * piece : width * (piece + 1)])
-                    if last:
-                        nc.sync.dma_start(out=out_rows[b, :, r, columns], in_=result[:, columns])
-            if not last:
-                nc.sync.dma_start(out=out_rows[b, :, r, :], in_=result[:])
+                nc.scalar.copy(out=result[:, N_TILE * n : N_TILE * (n + 1)], in_=acc[:])
+            nc.sync.dma_start(out=out_rows[b, :, r, :], in_=result[:])
 
         warm = psum_acc.tile([P, N_TILE], F32, name="acc")
         for k in range(WARM_UP):
@@ -207,24 +285,32 @@ def tile_denseattentiononehead_pa_kernel(
                 stop=True,
             )
 
-        transpose_tables(0)
-        copy_tables(0)
-        transpose_x(0)
+        nc.scalar.mul(out=tables[0][:, SIN, HALF:], in_=tables[0][:, SIN, HALF:], mul=-1.0)
+        transpose_tables(1)
+        copy_tables(1)
+        transpose_x(B)
         for step in range(TILES + 3):
-            if step < TILES:
+            if step < B:
+                multiply_in_rows(step)
+            elif step < TILES:
                 multiply_by_tables(step)
-            if 2 <= step < TILES:
+            if 2 <= step < TILES - 1:
                 quantise(step - 2)
-            if step < TILES - 1:
-                add_products(step, nc.gpsimd)
+            if step == TILES - 2:
+                quantise(TILES - 3)
             if step == TILES - 1:
                 quantise(TILES - 2)
-                add_products(TILES - 1, nc.vector)
-                quantise(TILES - 1)
-            if step + 1 < TILES:
+                add_and_quantise_last()
+            if B <= step < TILES - 1:
+                add_products(step)
+            if step < B:
+                transpose_and_add(step)
+            elif step + 1 < TILES:
                 transpose_x(step + 1)
-            if step % B == 0 and step // B + 1 < ROUNDS:
+            if step >= B and step % B == 0 and step // B + 1 < ROUNDS:
                 transpose_tables(step // B + 1)
                 copy_tables(step // B + 1)
-            if step >= 3:
+            if 3 <= step < TILES + 2:
                 project_and_store(step - 3)
+            elif step == TILES + 2:
+                project_and_store_last()

@@ -77,18 +77,21 @@ def tile_denseattentiononehead_pa_kernel(
             x_tiles[r, 0] = resident.tile([P, H], BF16, name="x%d_0" % r)
             x_tiles[r, 1] = resident.tile([P, H], BF16, name="x%d_1" % r)
             if r == 0:
+                for half in (slice(0, HALF), slice(HALF, H)):
+                    nc.sync.dma_start(out=x_tiles[0, 0][:, half], in_=x_rows[0, :, 0, half])
+                    nc.sync.dma_start(out=table[:, COS, half], in_=cos_rows[:, 0, half])
                 nc.sync.dma_start(out=table[:, SIN, HALF:], in_=sin_rows[:, r, :HALF])
                 nc.sync.dma_start(out=table[:, SIN, :HALF], in_=sin_rows[:, r, HALF:])
-                nc.sync.dma_start(out=table[:, COS, :], in_=cos_rows[:, r, :])
             else:
                 nc.sync.dma_start(out=table[:, COS, :], in_=cos_rows[:, r, :])
+                if r == 1:
+                    nc.sync.dma_start(out=x_tiles[0, 1][:], in_=x_rows[1, :, 0, :])
                 nc.sync.dma_start(out=table[:, SIN, :], in_=sin_rows[:, r, :])
-            nc.sync.dma_start(out=x_tiles[r, 0][:], in_=x_rows[0, :, r, :])
-            nc.sync.dma_start(out=x_tiles[r, 1][:], in_=x_rows[1, :, r, :])
+                nc.sync.dma_start(out=x_tiles[r, 0][:], in_=x_rows[0, :, r, :])
+                nc.sync.dma_start(out=x_tiles[r, 1][:], in_=x_rows[1, :, r, :])
             if r == 1:
                 load_weight()
 
-        table_banks = {}
         turned_tables = {}
         x_banks = {}
         products = {}
@@ -109,22 +112,20 @@ def tile_denseattentiononehead_pa_kernel(
                         stop=True,
                     )
 
-        def transpose_tables(r):
-            for kind in (COS, SIN):
-                bank = psum_tables.tile([P, PASSES, PAIRS, P], F32, name="table_t")
-                table_banks[r, kind] = bank
-                transpose_words(bank, tables[r][:, kind, :], False)
-
-        def copy_tables(r):
-            turned = stream.tile([P, 2, PASSES, P, PACK], BF16, name="turned")
-            turned_tables[r] = turned
-            bank = table_banks[r, COS]
-            target = turned[:, COS, :, :, :].rearrange("p g l t -> p (g l t)").bitcast(F32)
+        def turn_cos(r):
+            turned_tables[r] = stream.tile([P, 2, PASSES, P, PACK], BF16, name="turned")
+            bank = psum_tables.tile([P, PASSES, PAIRS, P], F32, name="table_t")
+            transpose_words(bank, tables[r][:, COS, :], False)
+            target = turned_tables[r][:, COS, :, :, :].rearrange("p g l t -> p (g l t)").bitcast(F32)
             nc.scalar.copy(
                 out=target.rearrange("p (g l u) -> p g l u", g=PASSES, u=PAIRS),
                 in_=bank[:].rearrange("p g u l -> p g l u"),
             )
-            bank = table_banks[r, SIN]
+
+        def turn_sin(r):
+            turned = turned_tables[r]
+            bank = psum_tables.tile([P, PASSES, PAIRS, P], F32, name="table_t")
+            transpose_words(bank, tables[r][:, SIN, :], False)
             nc.scalar.copy(
                 out=turned[:, SIN, 0, :, :].rearrange("p l t -> p (l t)").bitcast(F32).rearrange("p (l u) -> p l u", u=PAIRS),
                 in_=bank[:, 1, :, :].rearrange("p u l -> p l u"),
@@ -227,6 +228,20 @@ def tile_denseattentiononehead_pa_kernel(
                 op=MULT,
             )
 
+        def multiply_first_tile():
+            product = stream.tile([P, 2, PACK, WORDS], F32, name="product")
+            products[0] = product
+            for kind in (COS, SIN):
+                for g in range(PASSES):
+                    words = slice(P * g, P * (g + 1))
+                    columns = slice(HALF * g, HALF * (g + 1))
+                    nc.vector.tensor_tensor(
+                        out=product[:, kind, :, words],
+                        in0=x_tiles[0, 0][:, columns].rearrange("p (q t) -> p t q", t=PACK),
+                        in1=tables[0][:, kind, columns].rearrange("p (q t) -> p t q", t=PACK),
+                        op=MULT,
+                    )
+
         def transpose_and_add(i):
             product = products[i]
             grouped = stream.tile([P, PASSES, P, PACK], BF16, name="grouped", align_bytes=64)
@@ -286,11 +301,13 @@ def tile_denseattentiononehead_pa_kernel(
             )
 
         nc.scalar.mul(out=tables[0][:, SIN, HALF:], in_=tables[0][:, SIN, HALF:], mul=-1.0)
-        transpose_tables(1)
-        copy_tables(1)
+        turn_cos(1)
+        turn_sin(1)
         transpose_x(B)
         for step in range(TILES + 3):
-            if step < B:
+            if step == 0:
+                multiply_first_tile()
+            elif step < B:
                 multiply_in_rows(step)
             elif step < TILES:
                 multiply_by_tables(step)
@@ -303,13 +320,17 @@ def tile_denseattentiononehead_pa_kernel(
                 add_and_quantise_last()
             if B <= step < TILES - 1:
                 add_products(step)
+            if step == 1:
+                transpose_x(B + 1)
             if step < B:
                 transpose_and_add(step)
-            elif step + 1 < TILES:
+            elif B < step < TILES - 1:
                 transpose_x(step + 1)
-            if step >= B and step % B == 0 and step // B + 1 < ROUNDS:
-                transpose_tables(step // B + 1)
-                copy_tables(step // B + 1)
+            if step >= B and step // B + 1 < ROUNDS:
+                if step % B == 0:
+                    turn_cos(step // B + 1)
+                else:
+                    turn_sin(step // B + 1)
             if 3 <= step < TILES + 2:
                 project_and_store(step - 3)
             elif step == TILES + 2:

@@ -89,7 +89,7 @@ def tile_denseattentiononehead_pa_kernel(
                 nc.sync.dma_start(out=table[:, SIN, :], in_=sin_rows[:, r, :])
                 nc.sync.dma_start(out=x_tiles[r, 0][:], in_=x_rows[0, :, r, :])
                 nc.sync.dma_start(out=x_tiles[r, 1][:], in_=x_rows[1, :, r, :])
-            if r == 1:
+            if r == 2:
                 load_weight()
 
         turned_tables = {}
@@ -157,12 +157,17 @@ def tile_denseattentiononehead_pa_kernel(
                 op=MULT,
             )
 
+        def grouped_tile(i):
+            r, b = divmod(i, B)
+            if b == 0:
+                grouped_tiles[r] = stream.tile([P, B, PASSES, P, PACK], BF16, name="grouped", align_bytes=64)
+            return grouped_tiles[r][:, b, :, :, :]
+
         def add_products(i):
             product = products[i]
-            grouped = stream.tile([P, PASSES, P, PACK], BF16, name="grouped", align_bytes=64)
-            grouped_tiles[i] = grouped
+            grouped = grouped_tile(i)
             nc.gpsimd.tensor_tensor(
-                out=grouped[:].rearrange("p g l t -> p g (l t)"),
+                out=grouped.rearrange("p g l t -> p g (l t)"),
                 in0=product[:, COS, :].rearrange("p (g w) -> p g w", g=PASSES),
                 in1=product[:, SIN, :].rearrange("p (g w) -> p g w", g=PASSES)[:, ::-1, :],
                 op=ADD,
@@ -171,10 +176,9 @@ def tile_denseattentiononehead_pa_kernel(
 
         def add_and_quantise_last():
             i = TILES - 1
+            r, b = divmod(i, B)
             product = products[i]
-            grouped = stream.tile([P, PASSES, P, PACK], BF16, name="grouped", align_bytes=64)
-            codes[i] = stream.tile([P, PASSES * P], U32, name="codes", align_bytes=64)
-            scales[i] = stream.tile([P, PASSES * P], U8, name="scales", align_bytes=64)
+            grouped = grouped_tile(i)
             for g in range(PASSES):
                 nc.vector.tensor_tensor(
                     out=grouped[:, g, :, :].rearrange("p l t -> p (l t)"),
@@ -184,8 +188,8 @@ def tile_denseattentiononehead_pa_kernel(
                 )
             for g in range(PASSES):
                 nc.vector.quantize_mx(
-                    out=codes[i][:, P * g : P * (g + 1)].bitcast(FP8X4),
-                    scales=scales[i][:, P * g : P * (g + 1)],
+                    out=codes[r][:, b, P * g : P * (g + 1)].bitcast(FP8X4),
+                    scales=scales[r][:, b, P * g : P * (g + 1)],
                     in_=grouped[:, g, :, :].rearrange("p l t -> p (l t)"),
                 )
 
@@ -200,8 +204,8 @@ def tile_denseattentiononehead_pa_kernel(
                 for n in range(N_TILES):
                     nc.tensor.matmul_mx(
                         out=accs[n][:],
-                        lhsT=codes[i][:, P * g : P * (g + 1)].bitcast(FP8X4),
-                        lhsT_scale=scales[i][:, P * g : P * (g + 1)],
+                        lhsT=codes[r][:, b, P * g : P * (g + 1)].bitcast(FP8X4),
+                        lhsT_scale=scales[r][:, b, P * g : P * (g + 1)],
                         rhs=w_words[:, g, 2 * N_TILE * n : 2 * N_TILE * (n + 1)].bitcast(FP4X4),
                         rhs_scale=w_scales[:, g, N_TILE * n : N_TILE * (n + 1)],
                         start=(g == 0),
@@ -244,8 +248,7 @@ def tile_denseattentiononehead_pa_kernel(
 
         def transpose_and_add(i):
             product = products[i]
-            grouped = stream.tile([P, PASSES, P, PACK], BF16, name="grouped", align_bytes=64)
-            grouped_tiles[i] = grouped
+            grouped = grouped_tile(i)
             for g in range(PASSES):
                 own = slice(P * g, P * (g + 1))
                 other = slice(P * (1 - g), P * (2 - g))
@@ -263,13 +266,16 @@ def tile_denseattentiononehead_pa_kernel(
                 nc.scalar.copy(out=grouped[:, g, :, :], in_=h_t[:].rearrange("p t l -> p l t"))
 
 
-        def quantise(i):
-            codes[i] = stream.tile([P, PASSES * P], U32, name="codes", align_bytes=64)
-            scales[i] = stream.tile([P, PASSES * P], U8, name="scales", align_bytes=64)
+        def quantise(i, count):
+            r, b = divmod(i, B)
+            if b == 0:
+                codes[r] = stream.tile([P, B, PASSES * P], U32, name="codes", align_bytes=64)
+                scales[r] = stream.tile([P, B, PASSES * P], U8, name="scales", align_bytes=64)
+            tiles = slice(b, b + count)
             nc.vector.quantize_mx(
-                out=codes[i][:].bitcast(FP8X4),
-                scales=scales[i][:],
-                in_=grouped_tiles[i][:].rearrange("p g l t -> p (g l t)"),
+                out=codes[r][:, tiles, :].rearrange("p b w -> p (b w)").bitcast(FP8X4),
+                scales=scales[r][:, tiles, :].rearrange("p b w -> p (b w)"),
+                in_=grouped_tiles[r][:, tiles, :, :, :].rearrange("p b g l t -> p (b g l t)"),
             )
 
         def project_and_store(i):
@@ -280,8 +286,8 @@ def tile_denseattentiononehead_pa_kernel(
                 for g in range(PASSES):
                     nc.tensor.matmul_mx(
                         out=acc[:],
-                        lhsT=codes[i][:, P * g : P * (g + 1)].bitcast(FP8X4),
-                        lhsT_scale=scales[i][:, P * g : P * (g + 1)],
+                        lhsT=codes[r][:, b, P * g : P * (g + 1)].bitcast(FP8X4),
+                        lhsT_scale=scales[r][:, b, P * g : P * (g + 1)],
                         rhs=w_words[:, g, 2 * N_TILE * n : 2 * N_TILE * (n + 1)].bitcast(FP4X4),
                         rhs_scale=w_scales[:, g, N_TILE * n : N_TILE * (n + 1)],
                         start=(g == 0),
@@ -304,19 +310,21 @@ def tile_denseattentiononehead_pa_kernel(
         turn_cos(1)
         turn_sin(1)
         transpose_x(B)
-        for step in range(TILES + 3):
+        for step in range(TILES + 4):
             if step == 0:
                 multiply_first_tile()
             elif step < B:
                 multiply_in_rows(step)
             elif step < TILES:
                 multiply_by_tables(step)
-            if 2 <= step < TILES - 1:
-                quantise(step - 2)
+            if step == 3:
+                quantise(0, B)
+            elif 4 <= step < TILES - 1:
+                quantise(step - 2, 1)
             if step == TILES - 2:
-                quantise(TILES - 3)
+                quantise(TILES - 3, 1)
             if step == TILES - 1:
-                quantise(TILES - 2)
+                quantise(TILES - 2, 1)
                 add_and_quantise_last()
             if B <= step < TILES - 1:
                 add_products(step)
@@ -331,7 +339,7 @@ def tile_denseattentiononehead_pa_kernel(
                     turn_cos(step // B + 1)
                 else:
                     turn_sin(step // B + 1)
-            if 3 <= step < TILES + 2:
-                project_and_store(step - 3)
-            elif step == TILES + 2:
+            if 4 <= step < TILES + 3:
+                project_and_store(step - 4)
+            elif step == TILES + 3:
                 project_and_store_last()

@@ -94,6 +94,7 @@ def tile_denseattentiononehead_pa_kernel(
 
         turned_tables = {}
         x_banks = {}
+        x_ordered = {}
         products = {}
         grouped_tiles = {}
         codes = {}
@@ -139,9 +140,29 @@ def tile_denseattentiononehead_pa_kernel(
                 mul=-1.0,
             )
 
+        def order_x(i):
+            x_ordered[i] = stream.tile([P, PASSES, PAIRS, P], F32, name="x_ordered")
+            nc.scalar.copy(
+                out=x_ordered[i][:],
+                in_=x_tiles[divmod(i, B)][:].bitcast(F32).rearrange("p (g w u) -> p g u w", g=PASSES, u=PAIRS),
+            )
+
         def transpose_x(i):
-            x_banks[i] = psum_x.tile([P, PASSES, P, PAIRS], F32, name="x_t")
-            transpose_words(x_banks[i], x_tiles[divmod(i, B)][:], True)
+            bank = psum_x.tile([P, PASSES, P, PAIRS], F32, name="x_t")
+            x_banks[i] = bank
+            if i not in x_ordered:
+                transpose_words(bank, x_tiles[divmod(i, B)][:], True)
+                return
+            for g in range(PASSES):
+                for u in range(PAIRS):
+                    nc.tensor.matmul(
+                        out=bank[:, g, :, u],
+                        lhsT=x_ordered[i][:, g, u, :],
+                        rhs=identity[:],
+                        is_transpose=True,
+                        start=True,
+                        stop=True,
+                    )
 
         def multiply_by_tables(i):
             product = stream.tile([P, 2, H], F32, name="product")
@@ -317,9 +338,9 @@ def tile_denseattentiononehead_pa_kernel(
                 multiply_in_rows(step)
             elif step < TILES:
                 multiply_by_tables(step)
-            if step == 3:
-                quantise(0, B)
-            elif 4 <= step < TILES - 1:
+            if step in (4, 5):
+                quantise(B * (step - 4), B)
+            elif 6 <= step < TILES - 1:
                 quantise(step - 2, 1)
             if step == TILES - 2:
                 quantise(TILES - 3, 1)
@@ -328,18 +349,26 @@ def tile_denseattentiononehead_pa_kernel(
                 add_and_quantise_last()
             if B <= step < TILES - 1:
                 add_products(step)
-            if step == 1:
+            if 3 <= step and step + 2 < TILES:
+                order_x(step + 2)
+            if step == 0:
+                transpose_and_add(0)
                 transpose_x(B + 1)
-            if step < B:
-                transpose_and_add(step)
-            elif B < step < TILES - 1:
+            elif step == 1:
+                turn_cos(2)
+                turn_sin(2)
+                transpose_and_add(1)
+            elif 3 <= step < TILES - 1:
                 transpose_x(step + 1)
-            if step >= B and step // B + 1 < ROUNDS:
+            if step >= 4 and step // B + 1 < ROUNDS:
                 if step % B == 0:
                     turn_cos(step // B + 1)
                 else:
                     turn_sin(step // B + 1)
-            if 4 <= step < TILES + 3:
+            if step == 5:
+                project_and_store(0)
+                project_and_store(1)
+            elif 6 <= step < TILES + 3:
                 project_and_store(step - 4)
             elif step == TILES + 3:
                 project_and_store_last()

from contextlib import ExitStack

import concourse.mybir as mybir
from concourse.masks import make_identity

F32 = mybir.dt.float32
BF16 = mybir.dt.bfloat16
I32 = mybir.dt.int32
U32 = mybir.dt.uint32
U8 = mybir.dt.uint8
FP8X4 = mybir.dt.float8_e4m3fn_x4
FP4X4 = mybir.dt.float4_e2m1fn_x4
MULT = mybir.AluOpType.mult
ADD = mybir.AluOpType.add

B, L, H = 2, 1024, 1024
HALF = H // 2
P = 128
PACK = 4
PAIRS = PACK // 2
PASSES = H // (P * PACK)
N_TILE = 512
N_TILES = H // N_TILE
ROUNDS = L // P
TILES = ROUNDS * B
COS, SIN = 0, 1
WORDS = H // PACK
WARM_UP = 4

FLOPS = 2 * B * L * H * H


def tile_denseattentiononehead_pa_kernel(
    tc, hidden_states, W_q_words, W_q_scales, cos, sin, out
):
    nc = tc.nc

    x_rows = hidden_states.rearrange("b (p r) j -> b p r j", r=ROUNDS)
    cos_rows = cos.rearrange("(p r) j -> p r j", r=ROUNDS)
    sin_rows = sin.rearrange("(p r) j -> p r j", r=ROUNDS)
    out_rows = out.rearrange("b (p r) o -> b p r o", r=ROUNDS)

    with ExitStack() as ctx:
        resident = ctx.enter_context(tc.tile_pool(name="resident", bufs=1))
        stream = ctx.enter_context(tc.tile_pool(name="stream", bufs=4))
        results = ctx.enter_context(tc.tile_pool(name="results", bufs=6))
        psum_x = ctx.enter_context(tc.psum_pool(name="psum_x", bufs=2))
        psum_tables = ctx.enter_context(tc.psum_pool(name="psum_tables", bufs=2))
        psum_acc = ctx.enter_context(tc.psum_pool(name="psum_acc", bufs=4))
        ctx.enter_context(tc.manual_schedule())

        identity = resident.tile([P, P], F32)
        make_identity(nc, identity[:])

        w_words = resident.tile([P, PASSES, 2 * H], U8, align_bytes=64)
        w_scales = resident.tile([P, PASSES, H], U8, align_bytes=64)
        nc.vector.memset(w_scales[:].rearrange("p g n -> p (g n)").bitcast(I32), 0)

        def load_weight():
            nc.sync.dma_start(
                out=w_words[:].bitcast(I32),
                in_=W_q_words.rearrange("g p n -> p g n").bitcast(I32),
            )
            for quadrant in range(4):
                nc.sync.dma_start(
                    out=w_scales[32 * quadrant : 32 * quadrant + 4, :, :].bitcast(I32),
                    in_=W_q_scales[:, 4 * quadrant : 4 * quadrant + 4, :]
                    .rearrange("g q n -> q g n")
                    .bitcast(I32),
                )

        x_tiles = {}
        tables = {}
        for r in range(ROUNDS):
            table = resident.tile([P, 2, H], BF16, name="table%d" % r)
            tables[r] = table
            x_tiles[r, 0] = resident.tile([P, H], BF16, name="x%d_0" % r)
            x_tiles[r, 1] = resident.tile([P, H], BF16, name="x%d_1" % r)
            if r == 0:
                for half in (slice(0, HALF), slice(HALF, H)):
                    nc.sync.dma_start(out=x_tiles[0, 0][:, half], in_=x_rows[0, :, 0, half])
                    nc.sync.dma_start(out=table[:, COS, half], in_=cos_rows[:, 0, half])
                nc.sync.dma_start(out=table[:, SIN, HALF:], in_=sin_rows[:, r, :HALF])
                nc.sync.dma_start(out=table[:, SIN, :HALF], in_=sin_rows[:, r, HALF:])
            else:
                nc.sync.dma_start(out=table[:, COS, :], in_=cos_rows[:, r, :])
                if r == 1:
                    nc.sync.dma_start(out=x_tiles[0, 1][:], in_=x_rows[1, :, 0, :])
                nc.sync.dma_start(out=table[:, SIN, :], in_=sin_rows[:, r, :])
                nc.sync.dma_start(out=x_tiles[r, 0][:], in_=x_rows[0, :, r, :])
                nc.sync.dma_start(out=x_tiles[r, 1][:], in_=x_rows[1, :, r, :])
            if r == 2:
                load_weight()

        turned_tables = {}
        x_banks = {}
        x_ordered = {}
        products = {}
        grouped_tiles = {}
        codes = {}
        scales = {}

        def transpose_words(bank, rows, side_by_side):
            words = rows.bitcast(F32)
            for g in range(PASSES):
                for u in range(PAIRS):
                    nc.tensor.matmul(
                        out=bank[:, g, :, u] if side_by_side else bank[:, g, u, :],
                        lhsT=words[:, PAIRS * P * g + u : PAIRS * P * (g + 1) : PAIRS],
                        rhs=identity[:],
                        is_transpose=True,
                        start=True,
                        stop=True,
                    )

        def turn_cos(r):
            turned_tables[r] = stream.tile([P, 2, PASSES, P, PACK], BF16, name="turned")
            bank = psum_tables.tile([P, PASSES, PAIRS, P], F32, name="table_t")
            transpose_words(bank, tables[r][:, COS, :], False)
            target = turned_tables[r][:, COS, :, :, :].rearrange("p g l t -> p (g l t)").bitcast(F32)
            nc.scalar.copy(
                out=target.rearrange("p (g l u) -> p g l u", g=PASSES, u=PAIRS),
                in_=bank[:].rearrange("p g u l -> p g l u"),
            )

        def turn_sin(r):
            turned = turned_tables[r]
            bank = psum_tables.tile([P, PASSES, PAIRS, P], F32, name="table_t")
            transpose_words(bank, tables[r][:, SIN, :], False)
            nc.scalar.copy(
                out=turned[:, SIN, 0, :, :].rearrange("p l t -> p (l t)").bitcast(F32).rearrange("p (l u) -> p l u", u=PAIRS),
                in_=bank[:, 1, :, :].rearrange("p u l -> p l u"),
            )
            nc.scalar.mul(
                out=turned[:, SIN, 1, :, :].rearrange("p l (u e) -> p l u e", e=2),
                in_=bank[:, 0, :, :]
                .rearrange("p u l -> p (u l)")
                .bitcast(BF16)
                .rearrange("p (u l e) -> p l u e", u=PAIRS, e=2),
                mul=-1.0,
            )

        def order_x(i):
            x_ordered[i] = stream.tile([P, PASSES, PAIRS, P], F32, name="x_ordered")
            nc.scalar.copy(
                out=x_ordered[i][:],
                in_=x_tiles[divmod(i, B)][:].bitcast(F32).rearrange("p (g w u) -> p g u w", g=PASSES, u=PAIRS),
            )

        def transpose_x(i):
            bank = psum_x.tile([P, PASSES, P, PAIRS], F32, name="x_t")
            x_banks[i] = bank
            if i not in x_ordered:
                transpose_words(bank, x_tiles[divmod(i, B)][:], True)
                return
            for g in range(PASSES):
                for u in range(PAIRS):
                    nc.tensor.matmul(
                        out=bank[:, g, :, u],
                        lhsT=x_ordered[i][:, g, u, :],
                        rhs=identity[:],
                        is_transpose=True,
                        start=True,
                        stop=True,
                    )

        def multiply_by_tables(i):
            product = stream.tile([P, 2, H], F32, name="product")
            products[i] = product
            nc.vector.tensor_tensor(
                out=product[:],
                in0=x_banks[i][:]
                .rearrange("p g l u -> p (g l u)")
                .bitcast(BF16)
                .unsqueeze(1)
                .to_broadcast([P, 2, H]),
                in1=turned_tables[i // B][:].rearrange("p a g l t -> p a (g l t)"),
                op=MULT,
            )

        def grouped_tile(i):
            r, b = divmod(i, B)
            if b == 0:
                grouped_tiles[r] = stream.tile([P, B, PASSES, P, PACK], BF16, name="grouped", align_bytes=64)
            return grouped_tiles[r][:, b, :, :, :]

        def add_products(i):
            product = products[i]
            grouped = grouped_tile(i)
            nc.gpsimd.tensor_tensor(
                out=grouped.rearrange("p g l t -> p g (l t)"),
                in0=product[:, COS, :].rearrange("p (g w) -> p g w", g=PASSES),
                in1=product[:, SIN, :].rearrange("p (g w) -> p g w", g=PASSES)[:, ::-1, :],
                op=ADD,
            )


        def add_and_quantise_last():
            i = TILES - 1
            r, b = divmod(i, B)
            product = products[i]
            grouped = grouped_tile(i)
            for g in range(PASSES):
                nc.vector.tensor_tensor(
                    out=grouped[:, g, :, :].rearrange("p l t -> p (l t)"),
                    in0=product[:, COS, HALF * g : HALF * (g + 1)],
                    in1=product[:, SIN, HALF * (1 - g) : HALF * (2 - g)],
                    op=ADD,
                )
            for g in range(PASSES):
                nc.vector.quantize_mx(
                    out=codes[r][:, b, P * g : P * (g + 1)].bitcast(FP8X4),
                    scales=scales[r][:, b, P * g : P * (g + 1)],
                    in_=grouped[:, g, :, :].rearrange("p l t -> p (l t)"),
                )

        def project_and_store_last():
            i = TILES - 1
            r, b = divmod(i, B)
            result = results.tile([P, H], F32, name="result")
            accs = {}
            for n in range(N_TILES):
                accs[n] = psum_acc.tile([P, N_TILE], F32, name="acc")
            for g in range(PASSES):
                for n in range(N_TILES):
                    nc.tensor.matmul_mx(
                        out=accs[n][:],
                        lhsT=codes[r][:, b, P * g : P * (g + 1)].bitcast(FP8X4),
                        lhsT_scale=scales[r][:, b, P * g : P * (g + 1)],
                        rhs=w_words[:, g, 2 * N_TILE * n : 2 * N_TILE * (n + 1)].bitcast(FP4X4),
                        rhs_scale=w_scales[:, g, N_TILE * n : N_TILE * (n + 1)],
                        start=(g == 0),
                        stop=(g == PASSES - 1),
                    )
            for n, copy in ((0, nc.scalar.copy), (1, nc.vector.tensor_copy)):
                for piece in range(2):
                    width = N_TILE // 2
                    columns = slice(N_TILE * n + width * piece, N_TILE * n + width * (piece + 1))
                    copy(out=result[:, columns], in_=accs[n][:, width * piece : width * (piece + 1)])
                    nc.sync.dma_start(out=out_rows[b, :, r, columns], in_=result[:, columns])


        def multiply_in_rows(i):
            product = stream.tile([P, 2, PACK, WORDS], F32, name="product")
            products[i] = product
            nc.vector.tensor_tensor(
                out=product[:],
                in0=x_tiles[divmod(i, B)][:]
                .rearrange("p (q t) -> p t q", t=PACK)
                .unsqueeze(1)
                .to_broadcast([P, 2, PACK, WORDS]),
                in1=tables[i // B][:].rearrange("p a (q t) -> p a t q", t=PACK),
                op=MULT,
            )

        def multiply_first_tile():
            product = stream.tile([P, 2, PACK, WORDS], F32, name="product")
            products[0] = product
            for kind in (COS, SIN):
                for g in range(PASSES):
                    words = slice(P * g, P * (g + 1))
                    columns = slice(HALF * g, HALF * (g + 1))
                    nc.vector.tensor_tensor(
                        out=product[:, kind, :, words],
                        in0=x_tiles[0, 0][:, columns].rearrange("p (q t) -> p t q", t=PACK),
                        in1=tables[0][:, kind, columns].rearrange("p (q t) -> p t q", t=PACK),
                        op=MULT,
                    )

        def transpose_and_add(i):
            product = products[i]
            grouped = grouped_tile(i)
            for g in range(PASSES):
                own = slice(P * g, P * (g + 1))
                other = slice(P * (1 - g), P * (2 - g))
                h_t = psum_acc.tile([P, PACK, P], F32, name="acc")
                for t in range(PACK):
                    for kind, words in ((COS, own), (SIN, other)):
                        nc.tensor.matmul(
                            out=h_t[:, t, :],
                            lhsT=product[:, kind, t, words],
                            rhs=identity[:],
                            is_transpose=True,
                            start=(kind == COS),
                            stop=(kind == SIN),
                        )
                nc.scalar.copy(out=grouped[:, g, :, :], in_=h_t[:].rearrange("p t l -> p l t"))


        def quantise(i, count):
            r, b = divmod(i, B)
            if b == 0:
                codes[r] = stream.tile([P, B, PASSES * P], U32, name="codes", align_bytes=64)
                scales[r] = stream.tile([P, B, PASSES * P], U8, name="scales", align_bytes=64)
            tiles = slice(b, b + count)
            nc.vector.quantize_mx(
                out=codes[r][:, tiles, :].rearrange("p b w -> p (b w)").bitcast(FP8X4),
                scales=scales[r][:, tiles, :].rearrange("p b w -> p (b w)"),
                in_=grouped_tiles[r][:, tiles, :, :, :].rearrange("p b g l t -> p (b g l t)"),
            )

        def project_and_store(i):
            r, b = divmod(i, B)
            result = results.tile([P, H], F32, name="result")
            for n in range(N_TILES):
                acc = psum_acc.tile([P, N_TILE], F32, name="acc")
                for g in range(PASSES):
                    nc.tensor.matmul_mx(
                        out=acc[:],
                        lhsT=codes[r][:, b, P * g : P * (g + 1)].bitcast(FP8X4),
                        lhsT_scale=scales[r][:, b, P * g : P * (g + 1)],
                        rhs=w_words[:, g, 2 * N_TILE * n : 2 * N_TILE * (n + 1)].bitcast(FP4X4),
                        rhs_scale=w_scales[:, g, N_TILE * n : N_TILE * (n + 1)],
                        start=(g == 0),
                        stop=(g == PASSES - 1),
                    )
                nc.scalar.copy(out=result[:, N_TILE * n : N_TILE * (n + 1)], in_=acc[:])
            nc.sync.dma_start(out=out_rows[b, :, r, :], in_=result[:])

        warm = psum_acc.tile([P, N_TILE], F32, name="acc")
        for k in range(WARM_UP):
            nc.tensor.matmul(
                out=warm[:],
                lhsT=tables[0][:, COS, :P],
                rhs=tables[0][:, COS, :N_TILE],
                start=True,
                stop=True,
            )

        nc.scalar.mul(out=tables[0][:, SIN, HALF:], in_=tables[0][:, SIN, HALF:], mul=-1.0)
        turn_cos(1)
        turn_sin(1)
        transpose_x(B)
        for step in range(TILES + 4):
            if step == 0:
                multiply_first_tile()
            elif step < B:
                multiply_in_rows(step)
            elif step < TILES:
                multiply_by_tables(step)
            if step in (4, 5):
                quantise(B * (step - 4), B)
            elif 6 <= step < TILES - 1:
                quantise(step - 2, 1)
            if step == TILES - 2:
                quantise(TILES - 3, 1)
            if step == TILES - 1:
                quantise(TILES - 2, 1)
                add_and_quantise_last()
            if B <= step < TILES - 1:
                add_products(step)
            if 3 <= step and step + 2 < TILES:
                order_x(step + 2)
            if step == 0:
                transpose_and_add(0)
                transpose_x(B + 1)
            elif step == 1:
                turn_cos(2)
                turn_sin(2)
                transpose_and_add(1)
            elif 3 <= step < TILES - 1:
                transpose_x(step + 1)
            if step >= 4 and step // B + 1 < ROUNDS:
                if step % B == 0:
                    turn_cos(step // B + 1)
                else:
                    turn_sin(step // B + 1)
            if step == 5:
                project_and_store(0)
                project_and_store(1)
            elif 6 <= step < TILES + 3:
                project_and_store(step - 4)
            elif step == TILES + 3:
                project_and_store_last()
